import numpy as np
import ml_dtypes


def mxq(x, axis, fmt="e4m3"):
    dtype, down = {"e4m3": (ml_dtypes.float8_e4m3fn, 7), "e5m2": (ml_dtypes.float8_e5m2, 14)}[fmt]
    v = np.moveaxis(np.asarray(x, np.float32).astype(ml_dtypes.bfloat16).astype(np.float64), axis, -1)
    blocks = v.reshape(v.shape[:-1] + (-1, 32))
    amax = np.abs(blocks).max(-1, keepdims=True)
    byte = np.maximum(np.where(amax > 0, np.frexp(amax)[1] - 1 + 127, 0) - down, 1)
    scale = np.exp2(byte - 127.0)
    codes = (blocks / scale).astype(np.float32).astype(dtype).astype(np.float64)
    return np.moveaxis((codes * scale).reshape(v.shape), -1, axis)


WIDE = False


def mx_kscale(k):
    if not WIDE:
        return np.ones(k)
    levels = np.array([10, -10, 5, -5, 0])
    a = np.random.permutation(np.resize(levels, k // 512 * 4)).reshape(k // 512, 4)
    idx = np.arange(k)
    return np.exp2(a[idx // 512, idx % 128 // 32])


BF16 = ml_dtypes.bfloat16


def bf(x):
    return np.asarray(x, np.float32).astype(BF16)


def f64(x):
    return np.asarray(x).astype(np.float64)


B, L, DIMIN, WIDTH, N_HEADS, N_EMBDS = 8, 128, 512, 2048, 8, 64
EPS = 1e-6
XS = 10.0
SD = np.sqrt(DIMIN / WIDTH)


def setup_inputs():
    s = mx_kscale(WIDTH)
    t = mx_kscale(WIDTH)
    return {"o": bf(np.random.standard_normal((B, L, WIDTH)) * 0.6 * s),
            "o_w": bf(np.random.standard_normal((WIDTH, WIDTH)) * 0.5 / np.sqrt(WIDTH) / s[None, :] * t[:, None]),
            "o_b": bf(np.random.standard_normal(WIDTH) * 0.1 * t),
            "D": bf(np.random.standard_normal((WIDTH, DIMIN)) * SD / t[:, None]),
            "x": bf(np.random.standard_normal((B, L, DIMIN)) * XS)}


def reference(o, o_w, o_b, D, x):
    xc = f64(x)
    d_target = (mxq(f64(o), 2, "e4m3") @ mxq(f64(o_w), 1, "e4m3").T) + f64(o_b)
    z_pred_ = np.maximum(d_target, 0.0)
    Dz = mxq(z_pred_, 2, "e4m3") @ mxq(f64(D), 0, "e4m3")
    Dz_norm = np.sqrt(np.sum(Dz * Dz, axis=-1, keepdims=True)) + EPS
    proj_scale = np.sum(Dz * xc, axis=-1, keepdims=True) / np.square(Dz_norm)
    z_pred = z_pred_ * proj_scale
    x_pred = proj_scale * Dz
    return z_pred, x_pred

@@ -1,0 +1,276 @@
+from contextlib import ExitStack
+
+import concourse.mybir as mybir
+from concourse.masks import make_identity
+
+F32 = mybir.dt.float32
+BF16 = mybir.dt.bfloat16
+U32 = mybir.dt.uint32
+U8 = mybir.dt.uint8
+FP8X4 = mybir.dt.float8_e4m3fn_x4
+ACT = mybir.ActivationFunctionType
+ALU = mybir.AluOpType
+
+P = 128
+PACK = 4
+K_PASS = P * PACK
+ROWS = 1024
+WIDTH = 2048
+DIM = 512
+PASSES = WIDTH // K_PASS
+GROUPS = WIDTH // K_PASS
+PAIR = 2 * P
+W_PAIRS = WIDTH // PAIR
+EPS = 1e-6
+RAW_BUFS = 4
+CHUNKS = ((0, 512), (512, 256), (768, 256))
+FIRST_POST = 2
+
+FLOPS = 2 * ROWS * WIDTH * WIDTH + 2 * ROWS * WIDTH * DIM
+
+
+def tile_originaltemporalsae_pa_kernel(tc, o, o_w, o_b, D, x, out_0, out_1):
+    nc = tc.nc
+    o_rows = o.flatten_outer_dims()
+    x_rows = x.flatten_outer_dims()
+    z_rows = out_0.flatten_outer_dims()
+    xp_rows = out_1.flatten_outer_dims()
+
+    views = {}
+    for a in range(ROWS // PAIR):
+        views[("o", a)] = o_rows.rearrange("(a t p) k -> a p t k", t=2, p=P)[a]
+    for a in range(W_PAIRS):
+        views[("w", a)] = o_w.rearrange("(a p h t) k -> a h p t k", p=P, h=2, t=2)[a // 2, a % 2]
+    for a in range(GROUPS // 2):
+        views[("D", a)] = D.rearrange("(a g p j) n -> a p g (j n)", g=2, p=P, j=PACK)[a]
+    load_order = (
+        [("o", 0), ("o", 1)]
+        + [("w", a) for a in range(W_PAIRS)]
+        + [("D", 0), ("D", 1), ("o", 2), ("o", 3)]
+    )
+
+    with ExitStack() as ctx:
+        const = ctx.enter_context(tc.tile_pool(name="const", bufs=1))
+        raw_pool = ctx.enter_context(tc.tile_pool(name="raw", bufs=RAW_BUFS))
+        stage = ctx.enter_context(tc.tile_pool(name="stage", bufs=2))
+        relu_pool = ctx.enter_context(tc.tile_pool(name="relu", bufs=GROUPS))
+        out_pool = ctx.enter_context(tc.tile_pool(name="outp", bufs=4))
+        psum = ctx.enter_context(tc.psum_pool(name="psum", bufs=2))
+        ctx.enter_context(tc.manual_schedule())
+
+        w_codes = const.tile([P, PASSES, WIDTH], U32, align_bytes=64)
+        w_scales = const.tile([P, PASSES, WIDTH], U8, align_bytes=64)
+        o_codes = const.tile([P, PASSES, ROWS], U32, align_bytes=64)
+        o_scales = const.tile([P, PASSES, ROWS], U8, align_bytes=64)
+        d_codes = const.tile([P, GROUPS, DIM], U32, align_bytes=64)
+        d_scales = const.tile([P, GROUPS, DIM], U8, align_bytes=64)
+        x_sb = const.tile([P, ROWS // P, DIM], BF16)
+        ident = const.tile([P, P], F32)
+        bias_raw = const.tile([P, GROUPS, PACK], BF16)
+        bias = const.tile([P, GROUPS * PACK], F32)
+        eps = const.tile([P, 1], F32)
+        warm = const.tile([P, 1], F32)
+        sum_sq = const.tile([P, ROWS // P], F32)
+        norm = const.tile([P, ROWS // P], F32)
+        norm_sq = const.tile([P, ROWS // P], F32)
+        dot = const.tile([P, ROWS // P], F32)
+        inv = const.tile([P, ROWS // P], F32)
+        proj = const.tile([P, ROWS // P], F32)
+
+        raw_tiles = {}
+
+        def load_next():
+            if len(raw_tiles) < len(load_order):
+                key = load_order[len(raw_tiles)]
+                raw = raw_pool.tile([P, 2, WIDTH], BF16, tag="raw")
+                nc.sync.dma_start(out=raw[:], in_=views[key])
+                raw_tiles[key] = raw
+
+        def prepare_pair(key, codes, scales):
+            words = raw_tiles[key][:].bitcast(F32)
+            cols = slice(key[1] * PAIR, (key[1] + 1) * PAIR)
+            grouped = stage.tile([P, PASSES, PAIR, PACK], BF16, tag="grouped", align_bytes=64)
+            grouped_words = grouped[:].bitcast(F32)
+            for c in range(PASSES):
+                bank = psum.tile([P, 2, PAIR], F32, tag="tp", bufs=4)
+                for u in range(2):
+                    for t in range(2):
+                        nc.tensor.transpose(
+                            bank[:, u, t * P : (t + 1) * P],
+                            words[:, t, (2 * c + u) * P : (2 * c + u + 1) * P],
+                            ident[:],
+                        )
+                turned = bank[:].rearrange("q u m -> q m u")
+                if c % 2 == 0:
+                    nc.scalar.copy(out=grouped_words[:, c], in_=turned)
+                else:
+                    nc.vector.tensor_copy(out=grouped_words[:, c], in_=turned)
+            for c in range(PASSES):
+                nc.vector.quantize_mx(
+                    out=codes[:, c, cols].bitcast(FP8X4),
+                    scales=scales[:, c, cols],
+                    in_=grouped[:, c].rearrange("q m t -> q (m t)"),
+                )
+
+        def prepare_d(g):
+            raw = raw_tiles[("D", g // 2)]
+            grouped_d = stage.tile([P, DIM, PACK], BF16, tag="grouped_k", align_bytes=64)
+            nc.vector.tensor_copy(
+                out=grouped_d[:], in_=raw[:, g % 2].rearrange("p (j n) -> p n j", j=PACK)
+            )
+            nc.vector.quantize_mx(
+                out=d_codes[:, g].bitcast(FP8X4),
+                scales=d_scales[:, g],
+                in_=grouped_d[:].rearrange("p n j -> p (n j)"),
+            )
+
+        relu_t = {}
+        r_codes = {}
+        r_scales = {}
+
+        def stage1_pair(n, a):
+            row0, rows = CHUNKS[n]
+            g = a // 2
+            if a % 2 == 0:
+                r_tile = relu_pool.tile([P, PACK, rows], F32, tag="relu%d" % (n % 2))
+                relu_t[(n, g)] = r_tile
+            for t in range(2):
+                m = 2 * a + t
+                acc = psum.tile([P, rows], F32, tag="acc")
+                for c in range(PASSES):
+                    nc.tensor.matmul_mx(
+                        out=acc[:],
+                        lhsT=w_codes[:, c, m * P : (m + 1) * P].bitcast(FP8X4),
+                        lhsT_scale=w_scales[:, c, m * P : (m + 1) * P],
+                        rhs=o_codes[:, c, row0 : row0 + rows].bitcast(FP8X4),
+                        rhs_scale=o_scales[:, c, row0 : row0 + rows],
+                        start=(c == 0),
+                        stop=(c == PASSES - 1),
+                    )
+                nc.scalar.activation(
+                    out=relu_t[(n, g)][:, m % PACK],
+                    in_=acc[:],
+                    func=ACT.Relu,
+                    bias=bias[:, m : m + 1],
+                    scale=1.0,
+                )
+
+        def quantise_r(n, g):
+            rows = CHUNKS[n][1]
+            if g == 0:
+                codes = const.tile([P, GROUPS, rows], U32, tag="r_codes%d" % (n % 2), align_bytes=64)
+                scales = const.tile([P, GROUPS, rows], U8, tag="r_scales%d" % (n % 2), align_bytes=64)
+                r_codes[n] = codes
+                r_scales[n] = scales
+            grouped_r = stage.tile([P, rows, PACK], BF16, tag="grouped_k", align_bytes=64)
+            nc.vector.tensor_copy(
+                out=grouped_r[:], in_=relu_t[(n, g)][:].rearrange("p j r -> p r j")
+            )
+            nc.vector.quantize_mx(
+                out=r_codes[n][:, g].bitcast(FP8X4),
+                scales=r_scales[n][:, g],
+                in_=grouped_r[:].rearrange("p r j -> p (r j)"),
+            )
+
+        def stage2_tile(n, local):
+            i = CHUNKS[n][0] // P + local
+            here = slice(local * P, (local + 1) * P)
+            one = slice(i, i + 1)
+            dz = psum.tile([P, DIM], F32, tag="dz")
+            for g in range(GROUPS):
+                nc.tensor.matmul_mx(
+                    out=dz[:],
+                    lhsT=r_codes[n][:, g, here].bitcast(FP8X4),
+                    lhsT_scale=r_scales[n][:, g, here],
+                    rhs=d_codes[:, g].bitcast(FP8X4),
+                    rhs_scale=d_scales[:, g],
+                    start=(g == 0),
+                    stop=(g == GROUPS - 1),
+                )
+            squares = stage.tile([P, DIM], F32, tag="squares")
+            nc.scalar.activation(out=squares[:], in_=dz[:], func=ACT.Square, accum_out=sum_sq[:, one])
+            products = stage.tile([P, DIM], F32, tag="products")
+            nc.vector.scalar_tensor_tensor(
+                out=products[:],
+                in0=dz[:],
+                scalar=1.0,
+                in1=x_sb[:, i],
+                op0=ALU.mult,
+                op1=ALU.mult,
+                accum_out=dot[:, one],
+            )
+            nc.scalar.activation(out=norm[:, one], in_=sum_sq[:, one], func=ACT.Sqrt)
+            nc.scalar.activation(out=norm_sq[:, one], in_=norm[:, one], func=ACT.Square, bias=eps[:, 0:1])
+            nc.vector.reciprocal(out=inv[:, one], in_=norm_sq[:, one])
+            nc.vector.tensor_tensor(out=proj[:, one], in0=dot[:, one], in1=inv[:, one], op=ALU.mult)
+            x_pred = out_pool.tile([P, DIM], F32, tag="x_pred", bufs=2)
+            nc.vector.tensor_scalar(
+                out=x_pred[:], in0=dz[:], scalar1=proj[:, one], scalar2=None, op0=ALU.mult
+            )
+            nc.sync.dma_start(out=xp_rows[i * P : (i + 1) * P, :], in_=x_pred[:])
+
+        def z_tile(n, local):
+            i = CHUNKS[n][0] // P + local
+            here = slice(local * P, (local + 1) * P)
+            one = slice(i, i + 1)
+            for half in range(GROUPS // 2):
+                z_sb = out_pool.tile([P, 2, P, PACK], F32, tag="z_sb")
+                for s in range(2):
+                    g = 2 * half + s
+                    bank = psum.tile([P, PACK, P], F32, tag="tp", bufs=4)
+                    for j in range(PACK):
+                        nc.tensor.transpose(bank[:, j], relu_t[(n, g)][:, j, here], ident[:])
+                    turned = bank[:].rearrange("r j p -> r p j")
+                    if s == 0:
+                        nc.scalar.activation(out=z_sb[:, s], in_=turned, func=ACT.Copy, scale=proj[:, one])
+                    else:
+                        nc.vector.tensor_scalar(
+                            out=z_sb[:, s], in0=turned, scalar1=proj[:, one], scalar2=None, op0=ALU.mult
+                        )
+                nc.sync.dma_start(
+                    out=z_rows[i * P : (i + 1) * P, half * 2 * K_PASS : (half + 1) * 2 * K_PASS],
+                    in_=z_sb[:].rearrange("r s p j -> r (s p j)"),
+                )
+
+        for k in range(RAW_BUFS):
+            load_next()
+        nc.scalar.dma_start(out=bias_raw[:], in_=o_b.rearrange("(g p j) -> p g j", p=P, j=PACK))
+        make_identity(nc, ident[:])
+        nc.vector.memset(eps[:], EPS)
+        nc.scalar.activation(out=warm[:], in_=eps[:], func=ACT.Sqrt)
+        nc.vector.tensor_copy(out=bias[:], in_=bias_raw[:].rearrange("p g j -> p (g j)"))
+
+        steps = [("o", 0), ("o", 1)] + [("w", a) for a in range(W_PAIRS)] + [("o", 2), ("o", 3)]
+        for k, key in enumerate(steps):
+            if key[0] == "o":
+                prepare_pair(key, o_codes, o_scales)
+            else:
+                prepare_pair(key, w_codes, w_scales)
+            load_next()
+            before = steps[k - 1] if k > 0 else ("o", 0)
+            before2 = steps[k - 2] if k > 1 else ("o", 0)
+            if before2[0] == "w" and before2[1] % 2 == 1:
+                quantise_r(0, before2[1] // 2)
+            if k >= len(steps) - GROUPS:
+                prepare_d(k - (len(steps) - GROUPS))
+            if before[0] == "w":
+                stage1_pair(0, before[1])
+        nc.sync.dma_start(out=x_sb[:], in_=x_rows.rearrange("(t p) n -> p t n", p=P))
+
+        for n in range(1, len(CHUNKS)):
+            tiles_before = CHUNKS[n - 1][1] // P
+            for a in range(W_PAIRS):
+                stage1_pair(n, a)
+                if a % 2 == 0 and a > 0:
+                    quantise_r(n, a // 2 - 1)
+                if 0 <= a - FIRST_POST < tiles_before:
+                    stage2_tile(n - 1, a - FIRST_POST)
+                if 0 <= a - FIRST_POST - 2 < tiles_before:
+                    z_tile(n - 1, a - FIRST_POST - 2)
+            quantise_r(n, GROUPS - 1)
+
+        last = len(CHUNKS) - 1
+        for local in range(CHUNKS[last][1] // P):
+            stage2_tile(last, local)
+        for local in range(CHUNKS[last][1] // P):
+            z_tile(last, local)

@@ -115,8 +115,13 @@ def tile_originaltemporalsae_pa_kernel(tc, o, o_w, o_b, D, x, out_0, out_1):
         def prepare_d(g):
             raw = raw_tiles[("D", g // 2)]
             grouped_d = stage.tile([P, DIM, PACK], BF16, tag="grouped_k", align_bytes=64)
-            nc.vector.tensor_copy(
-                out=grouped_d[:], in_=raw[:, g % 2].rearrange("p (j n) -> p n j", j=PACK)
+            nc.gpsimd.tensor_scalar(
+                out=grouped_d[:],
+                in0=raw[:, g % 2].rearrange("p (j n) -> p n j", j=PACK),
+                scalar1=1.0,
+                scalar2=0.0,
+                op0=ALU.mult,
+                op1=ALU.add,
             )
             nc.vector.quantize_mx(
                 out=d_codes[:, g].bitcast(FP8X4),
@@ -163,8 +168,13 @@ def tile_originaltemporalsae_pa_kernel(tc, o, o_w, o_b, D, x, out_0, out_1):
                 r_codes[n] = codes
                 r_scales[n] = scales
             grouped_r = stage.tile([P, rows, PACK], BF16, tag="grouped_k", align_bytes=64)
-            nc.vector.tensor_copy(
-                out=grouped_r[:], in_=relu_t[(n, g)][:].rearrange("p j r -> p r j")
+            nc.gpsimd.tensor_scalar(
+                out=grouped_r[:],
+                in0=relu_t[(n, g)][:].rearrange("p j r -> p r j"),
+                scalar1=1.0,
+                scalar2=0.0,
+                op0=ALU.mult,
+                op1=ALU.add,
             )
             nc.vector.quantize_mx(
                 out=r_codes[n][:, g].bitcast(FP8X4),

@@ -23,6 +23,7 @@ PAIR = 2 * P
 W_PAIRS = WIDTH // PAIR
 EPS = 1e-6
 RAW_BUFS = 4
+RUN = 4
 CHUNKS = ((0, 512), (512, 256), (768, 256))
 FIRST_POST = 2
 
@@ -101,7 +102,7 @@ def tile_originaltemporalsae_pa_kernel(tc, o, o_w, o_b, D, x, out_0, out_1):
                             ident[:],
                         )
                 turned = bank[:].rearrange("q u m -> q m u")
-                if c % 2 == 0:
+                if c < PASSES - 1:
                     nc.scalar.copy(out=grouped_words[:, c], in_=turned)
                 else:
                     nc.vector.tensor_copy(out=grouped_words[:, c], in_=turned)
@@ -115,13 +116,9 @@ def tile_originaltemporalsae_pa_kernel(tc, o, o_w, o_b, D, x, out_0, out_1):
         def prepare_d(g):
             raw = raw_tiles[("D", g // 2)]
             grouped_d = stage.tile([P, DIM, PACK], BF16, tag="grouped_k", align_bytes=64)
-            nc.gpsimd.tensor_scalar(
-                out=grouped_d[:],
-                in0=raw[:, g % 2].rearrange("p (j n) -> p n j", j=PACK),
-                scalar1=1.0,
-                scalar2=0.0,
-                op0=ALU.mult,
-                op1=ALU.add,
+            nc.vector.tensor_copy(
+                out=grouped_d[:].rearrange("p (c i) j -> p c j i", i=RUN),
+                in_=raw[:, g % 2].rearrange("p (j c i) -> p c j i", j=PACK, i=RUN),
             )
             nc.vector.quantize_mx(
                 out=d_codes[:, g].bitcast(FP8X4),
@@ -168,13 +165,9 @@ def tile_originaltemporalsae_pa_kernel(tc, o, o_w, o_b, D, x, out_0, out_1):
                 r_codes[n] = codes
                 r_scales[n] = scales
             grouped_r = stage.tile([P, rows, PACK], BF16, tag="grouped_k", align_bytes=64)
-            nc.gpsimd.tensor_scalar(
-                out=grouped_r[:],
-                in0=relu_t[(n, g)][:].rearrange("p j r -> p r j"),
-                scalar1=1.0,
-                scalar2=0.0,
-                op0=ALU.mult,
-                op1=ALU.add,
+            nc.vector.tensor_copy(
+                out=grouped_r[:].rearrange("p (c i) j -> p c j i", i=RUN),
+                in_=relu_t[(n, g)][:].rearrange("p j (c i) -> p c j i", i=RUN),
             )
             nc.vector.quantize_mx(
                 out=r_codes[n][:, g].bitcast(FP8X4),
@@ -214,9 +207,7 @@ def tile_originaltemporalsae_pa_kernel(tc, o, o_w, o_b, D, x, out_0, out_1):
             nc.vector.reciprocal(out=inv[:, one], in_=norm_sq[:, one])
             nc.vector.tensor_tensor(out=proj[:, one], in0=dot[:, one], in1=inv[:, one], op=ALU.mult)
             x_pred = out_pool.tile([P, DIM], F32, tag="x_pred", bufs=2)
-            nc.vector.tensor_scalar(
-                out=x_pred[:], in0=dz[:], scalar1=proj[:, one], scalar2=None, op0=ALU.mult
-            )
+            nc.scalar.activation(out=x_pred[:], in_=dz[:], func=ACT.Copy, scale=proj[:, one])
             nc.sync.dma_start(out=xp_rows[i * P : (i + 1) * P, :], in_=x_pred[:])
 
         def z_tile(n, local):

from contextlib import ExitStack

import concourse.mybir as mybir
from concourse.masks import make_identity

F32 = mybir.dt.float32
BF16 = mybir.dt.bfloat16
U32 = mybir.dt.uint32
U8 = mybir.dt.uint8
FP8X4 = mybir.dt.float8_e4m3fn_x4
ACT = mybir.ActivationFunctionType
ALU = mybir.AluOpType

P = 128
PACK = 4
K_PASS = P * PACK
ROWS = 1024
WIDTH = 2048
DIM = 512
PASSES = WIDTH // K_PASS
GROUPS = WIDTH // K_PASS
PAIR = 2 * P
W_PAIRS = WIDTH // PAIR
EPS = 1e-6
RAW_BUFS = 4
RUN = 4
CHUNKS = ((0, 512), (512, 256), (768, 256))
FIRST_POST = 2

FLOPS = 2 * ROWS * WIDTH * WIDTH + 2 * ROWS * WIDTH * DIM


def tile_originaltemporalsae_pa_kernel(tc, o, o_w, o_b, D, x, out_0, out_1):
    nc = tc.nc
    o_rows = o.flatten_outer_dims()
    x_rows = x.flatten_outer_dims()
    z_rows = out_0.flatten_outer_dims()
    xp_rows = out_1.flatten_outer_dims()

    views = {}
    for a in range(ROWS // PAIR):
        views[("o", a)] = o_rows.rearrange("(a t p) k -> a p t k", t=2, p=P)[a]
    for a in range(W_PAIRS):
        views[("w", a)] = o_w.rearrange("(a p h t) k -> a h p t k", p=P, h=2, t=2)[a // 2, a % 2]
    for a in range(GROUPS // 2):
        views[("D", a)] = D.rearrange("(a g p j) n -> a p g (j n)", g=2, p=P, j=PACK)[a]
    load_order = (
        [("o", 0), ("o", 1)]
        + [("w", a) for a in range(W_PAIRS)]
        + [("D", 0), ("D", 1), ("o", 2), ("o", 3)]
    )

    with ExitStack() as ctx:
        const = ctx.enter_context(tc.tile_pool(name="const", bufs=1))
        raw_pool = ctx.enter_context(tc.tile_pool(name="raw", bufs=RAW_BUFS))
        stage = ctx.enter_context(tc.tile_pool(name="stage", bufs=2))
        relu_pool = ctx.enter_context(tc.tile_pool(name="relu", bufs=GROUPS))
        out_pool = ctx.enter_context(tc.tile_pool(name="outp", bufs=4))
        psum = ctx.enter_context(tc.psum_pool(name="psum", bufs=2))
        ctx.enter_context(tc.manual_schedule())

        w_codes = const.tile([P, PASSES, WIDTH], U32, align_bytes=64)
        w_scales = const.tile([P, PASSES, WIDTH], U8, align_bytes=64)
        o_codes = const.tile([P, PASSES, ROWS], U32, align_bytes=64)
        o_scales = const.tile([P, PASSES, ROWS], U8, align_bytes=64)
        d_codes = const.tile([P, GROUPS, DIM], U32, align_bytes=64)
        d_scales = const.tile([P, GROUPS, DIM], U8, align_bytes=64)
        x_sb = const.tile([P, ROWS // P, DIM], BF16)
        ident = const.tile([P, P], F32)
        bias_raw = const.tile([P, GROUPS, PACK], BF16)
        bias = const.tile([P, GROUPS * PACK], F32)
        eps = const.tile([P, 1], F32)
        warm = const.tile([P, 1], F32)
        sum_sq = const.tile([P, ROWS // P], F32)
        norm = const.tile([P, ROWS // P], F32)
        norm_sq = const.tile([P, ROWS // P], F32)
        dot = const.tile([P, ROWS // P], F32)
        inv = const.tile([P, ROWS // P], F32)
        proj = const.tile([P, ROWS // P], F32)

        raw_tiles = {}

        def load_next():
            if len(raw_tiles) < len(load_order):
                key = load_order[len(raw_tiles)]
                raw = raw_pool.tile([P, 2, WIDTH], BF16, tag="raw")
                nc.sync.dma_start(out=raw[:], in_=views[key])
                raw_tiles[key] = raw

        def prepare_pair(key, codes, scales):
            words = raw_tiles[key][:].bitcast(F32)
            cols = slice(key[1] * PAIR, (key[1] + 1) * PAIR)
            grouped = stage.tile([P, PASSES, PAIR, PACK], BF16, tag="grouped", align_bytes=64)
            grouped_words = grouped[:].bitcast(F32)
            for c in range(PASSES):
                bank = psum.tile([P, 2, PAIR], F32, tag="tp", bufs=4)
                for u in range(2):
                    for t in range(2):
                        nc.tensor.transpose(
                            bank[:, u, t * P : (t + 1) * P],
                            words[:, t, (2 * c + u) * P : (2 * c + u + 1) * P],
                            ident[:],
                        )
                turned = bank[:].rearrange("q u m -> q m u")
                if c < PASSES - 1:
                    nc.scalar.copy(out=grouped_words[:, c], in_=turned)
                else:
                    nc.vector.tensor_copy(out=grouped_words[:, c], in_=turned)
            for c in range(PASSES):
                nc.vector.quantize_mx(
                    out=codes[:, c, cols].bitcast(FP8X4),
                    scales=scales[:, c, cols],
                    in_=grouped[:, c].rearrange("q m t -> q (m t)"),
                )

        def prepare_d(g):
            raw = raw_tiles[("D", g // 2)]
            grouped_d = stage.tile([P, DIM, PACK], BF16, tag="grouped_k", align_bytes=64)
            nc.vector.tensor_copy(
                out=grouped_d[:].rearrange("p (c i) j -> p c j i", i=RUN),
                in_=raw[:, g % 2].rearrange("p (j c i) -> p c j i", j=PACK, i=RUN),
            )
            nc.vector.quantize_mx(
                out=d_codes[:, g].bitcast(FP8X4),
                scales=d_scales[:, g],
                in_=grouped_d[:].rearrange("p n j -> p (n j)"),
            )

        relu_t = {}
        r_codes = {}
        r_scales = {}

        def stage1_pair(n, a):
            row0, rows = CHUNKS[n]
            g = a // 2
            if a % 2 == 0:
                r_tile = relu_pool.tile([P, PACK, rows], F32, tag="relu%d" % (n % 2))
                relu_t[(n, g)] = r_tile
            for t in range(2):
                m = 2 * a + t
                acc = psum.tile([P, rows], F32, tag="acc")
                for c in range(PASSES):
                    nc.tensor.matmul_mx(
                        out=acc[:],
                        lhsT=w_codes[:, c, m * P : (m + 1) * P].bitcast(FP8X4),
                        lhsT_scale=w_scales[:, c, m * P : (m + 1) * P],
                        rhs=o_codes[:, c, row0 : row0 + rows].bitcast(FP8X4),
                        rhs_scale=o_scales[:, c, row0 : row0 + rows],
                        start=(c == 0),
                        stop=(c == PASSES - 1),
                    )
                nc.scalar.activation(
                    out=relu_t[(n, g)][:, m % PACK],
                    in_=acc[:],
                    func=ACT.Relu,
                    bias=bias[:, m : m + 1],
                    scale=1.0,
                )

        def quantise_r(n, g):
            rows = CHUNKS[n][1]
            if g == 0:
                codes = const.tile([P, GROUPS, rows], U32, tag="r_codes%d" % (n % 2), align_bytes=64)
                scales = const.tile([P, GROUPS, rows], U8, tag="r_scales%d" % (n % 2), align_bytes=64)
                r_codes[n] = codes
                r_scales[n] = scales
            grouped_r = stage.tile([P, rows, PACK], BF16, tag="grouped_k", align_bytes=64)
            nc.vector.tensor_copy(
                out=grouped_r[:].rearrange("p (c i) j -> p c j i", i=RUN),
                in_=relu_t[(n, g)][:].rearrange("p j (c i) -> p c j i", i=RUN),
            )
            nc.vector.quantize_mx(
                out=r_codes[n][:, g].bitcast(FP8X4),
                scales=r_scales[n][:, g],
                in_=grouped_r[:].rearrange("p r j -> p (r j)"),
            )

        def stage2_tile(n, local):
            i = CHUNKS[n][0] // P + local
            here = slice(local * P, (local + 1) * P)
            one = slice(i, i + 1)
            dz = psum.tile([P, DIM], F32, tag="dz")
            for g in range(GROUPS):
                nc.tensor.matmul_mx(
                    out=dz[:],
                    lhsT=r_codes[n][:, g, here].bitcast(FP8X4),
                    lhsT_scale=r_scales[n][:, g, here],
                    rhs=d_codes[:, g].bitcast(FP8X4),
                    rhs_scale=d_scales[:, g],
                    start=(g == 0),
                    stop=(g == GROUPS - 1),
                )
            squares = stage.tile([P, DIM], F32, tag="squares")
            nc.scalar.activation(out=squares[:], in_=dz[:], func=ACT.Square, accum_out=sum_sq[:, one])
            products = stage.tile([P, DIM], F32, tag="products")
            nc.vector.scalar_tensor_tensor(
                out=products[:],
                in0=dz[:],
                scalar=1.0,
                in1=x_sb[:, i],
                op0=ALU.mult,
                op1=ALU.mult,
                accum_out=dot[:, one],
            )
            nc.scalar.activation(out=norm[:, one], in_=sum_sq[:, one], func=ACT.Sqrt)
            nc.scalar.activation(out=norm_sq[:, one], in_=norm[:, one], func=ACT.Square, bias=eps[:, 0:1])
            nc.vector.reciprocal(out=inv[:, one], in_=norm_sq[:, one])
            nc.vector.tensor_tensor(out=proj[:, one], in0=dot[:, one], in1=inv[:, one], op=ALU.mult)
            x_pred = out_pool.tile([P, DIM], F32, tag="x_pred", bufs=2)
            nc.scalar.activation(out=x_pred[:], in_=dz[:], func=ACT.Copy, scale=proj[:, one])
            nc.sync.dma_start(out=xp_rows[i * P : (i + 1) * P, :], in_=x_pred[:])

        def z_tile(n, local):
            i = CHUNKS[n][0] // P + local
            here = slice(local * P, (local + 1) * P)
            one = slice(i, i + 1)
            for half in range(GROUPS // 2):
                z_sb = out_pool.tile([P, 2, P, PACK], F32, tag="z_sb")
                for s in range(2):
                    g = 2 * half + s
                    bank = psum.tile([P, PACK, P], F32, tag="tp", bufs=4)
                    for j in range(PACK):
                        nc.tensor.transpose(bank[:, j], relu_t[(n, g)][:, j, here], ident[:])
                    turned = bank[:].rearrange("r j p -> r p j")
                    if s == 0:
                        nc.scalar.activation(out=z_sb[:, s], in_=turned, func=ACT.Copy, scale=proj[:, one])
                    else:
                        nc.vector.tensor_scalar(
                            out=z_sb[:, s], in0=turned, scalar1=proj[:, one], scalar2=None, op0=ALU.mult
                        )
                nc.sync.dma_start(
                    out=z_rows[i * P : (i + 1) * P, half * 2 * K_PASS : (half + 1) * 2 * K_PASS],
                    in_=z_sb[:].rearrange("r s p j -> r (s p j)"),
                )

        for k in range(RAW_BUFS):
            load_next()
        nc.scalar.dma_start(out=bias_raw[:], in_=o_b.rearrange("(g p j) -> p g j", p=P, j=PACK))
        make_identity(nc, ident[:])
        nc.vector.memset(eps[:], EPS)
        nc.scalar.activation(out=warm[:], in_=eps[:], func=ACT.Sqrt)
        nc.vector.tensor_copy(out=bias[:], in_=bias_raw[:].rearrange("p g j -> p (g j)"))

        steps = [("o", 0), ("o", 1)] + [("w", a) for a in range(W_PAIRS)] + [("o", 2), ("o", 3)]
        for k, key in enumerate(steps):
            if key[0] == "o":
                prepare_pair(key, o_codes, o_scales)
            else:
                prepare_pair(key, w_codes, w_scales)
            load_next()
            before = steps[k - 1] if k > 0 else ("o", 0)
            before2 = steps[k - 2] if k > 1 else ("o", 0)
            if before2[0] == "w" and before2[1] % 2 == 1:
                quantise_r(0, before2[1] // 2)
            if k >= len(steps) - GROUPS:
                prepare_d(k - (len(steps) - GROUPS))
            if before[0] == "w":
                stage1_pair(0, before[1])
        nc.sync.dma_start(out=x_sb[:], in_=x_rows.rearrange("(t p) n -> p t n", p=P))

        for n in range(1, len(CHUNKS)):
            tiles_before = CHUNKS[n - 1][1] // P
            for a in range(W_PAIRS):
                stage1_pair(n, a)
                if a % 2 == 0 and a > 0:
                    quantise_r(n, a // 2 - 1)
                if 0 <= a - FIRST_POST < tiles_before:
                    stage2_tile(n - 1, a - FIRST_POST)
                if 0 <= a - FIRST_POST - 2 < tiles_before:
                    z_tile(n - 1, a - FIRST_POST - 2)
            quantise_r(n, GROUPS - 1)

        last = len(CHUNKS) - 1
        for local in range(CHUNKS[last][1] // P):
            stage2_tile(last, local)
        for local in range(CHUNKS[last][1] // P):
            z_tile(last, local)
